import numpy as np
import ml_dtypes


def mxq(x, axis, fmt="e4m3"):
    dtype, down = {"e4m3": (ml_dtypes.float8_e4m3fn, 7), "e5m2": (ml_dtypes.float8_e5m2, 14)}[fmt]
    v = np.moveaxis(np.asarray(x, np.float32).astype(ml_dtypes.bfloat16).astype(np.float64), axis, -1)
    blocks = v.reshape(v.shape[:-1] + (-1, 32))
    amax = np.abs(blocks).max(-1, keepdims=True)
    byte = np.maximum(np.where(amax > 0, np.frexp(amax)[1] - 1 + 127, 0) - down, 1)
    scale = np.exp2(byte - 127.0)
    codes = (blocks / scale).astype(np.float32).astype(dtype).astype(np.float64)
    return np.moveaxis((codes * scale).reshape(v.shape), -1, axis)


WIDE = False


def mx_kscale(k):
    if not WIDE:
        return np.ones(k)
    levels = np.array([10, -10, 5, -5, 0])
    a = np.random.permutation(np.resize(levels, k // 512 * 4)).reshape(k // 512, 4)
    idx = np.arange(k)
    return np.exp2(a[idx // 512, idx % 128 // 32])


BF16 = ml_dtypes.bfloat16


def bf(x):
    return np.asarray(x, np.float32).astype(BF16)


def f64(x):
    return np.asarray(x).astype(np.float64)


N, IN_DIM, HID, OUT_DIM = 4096, 512, 128, 256


def setup_inputs():
    s = mx_kscale(IN_DIM)
    return {"X": bf(np.random.standard_normal((N, IN_DIM)) * s),
            "A": bf(np.random.uniform(0.0, 1.0, (N, N)) * 0.5 / np.sqrt(N)),
            "W_in": bf(np.random.standard_normal((IN_DIM, HID)) / np.sqrt(IN_DIM) / s[:, None]),
            "b_in": bf(np.random.standard_normal(HID) * 0.1),
            "eps0": bf(np.random.uniform(0.2, 0.4, (1,)))}


def reference(X, A, W_in, b_in, eps0):
    h = (mxq(f64(X), 1, "e4m3") @ mxq(f64(W_in), 0, "e4m3")) + f64(b_in)
    return (mxq(f64(A), 1, "e4m3") @ mxq(h, 0, "e4m3")) + (1.0 + f64(eps0)) * h

@@ -1,0 +1,212 @@
+from contextlib import ExitStack
+
+import concourse.mybir as mybir
+from concourse.masks import make_identity
+
+F32 = mybir.dt.float32
+BF16 = mybir.dt.bfloat16
+U32 = mybir.dt.uint32
+U8 = mybir.dt.uint8
+FP8X4 = mybir.dt.float8_e4m3fn_x4
+ADD = mybir.AluOpType.add
+MULT = mybir.AluOpType.mult
+
+P = 128
+NODES, FEATS, HID = 4096, 512, 128
+PACK = 4
+K_PASS = P * PACK
+PASSES = NODES // K_PASS
+SLAB_K = 4096
+SLAB_OPERANDS = SLAB_K // K_PASS
+SLAB_BANKS = 4
+X_SLABS = NODES * FEATS // (P * SLAB_K)
+A_SLABS = NODES // P
+SLABS = X_SLABS + A_SLABS
+A_LOADS = A_SLABS // 2
+A_AHEAD = 4
+VECTOR_BANK = 1
+
+FLOPS = 2 * NODES * FEATS * HID + 2 * NODES * NODES * HID
+
+
+def tile_gin_pa_t_kernel(tc, X, A, W_in, b_in, eps0, out):
+    nc = tc.nc
+
+    x_view = X.rearrange("(x c p e) k -> x p c (e k)", c=4, p=P, e=2)
+    a_view = A.rearrange("(c p e) k -> c p (e k)", p=P, e=2)
+    w_view = W_in.rearrange("(u q e) n -> q u (e n)", u=2, q=P, e=2)
+    out_view = out.rearrange("(g u p e) n -> g p u (e n)", u=2, p=P, e=2)
+
+    with ExitStack() as ctx:
+        keep = ctx.enter_context(tc.tile_pool(name="keep", bufs=1))
+        x_pool = ctx.enter_context(tc.tile_pool(name="x_pool", bufs=X_SLABS))
+        a_pool = ctx.enter_context(tc.tile_pool(name="a_pool", bufs=A_AHEAD + 1))
+        grouped_pool = ctx.enter_context(tc.tile_pool(name="grouped_pool", bufs=3))
+        packed_pool = ctx.enter_context(tc.tile_pool(name="packed_pool", bufs=4))
+        out_pool = ctx.enter_context(tc.tile_pool(name="out_pool", bufs=3))
+        tr_psum = ctx.enter_context(tc.psum_pool(name="tr_psum", bufs=6))
+        mx_psum = ctx.enter_context(tc.psum_pool(name="mx_psum", bufs=2))
+        ctx.enter_context(tc.manual_schedule())
+
+        w_raw = keep.tile([P, PACK, HID], BF16)
+        nc.scalar.dma_start(out=w_raw[:].rearrange("q (u e) n -> q u (e n)", u=2), in_=w_view)
+        bias_bf = keep.tile([P, HID], BF16)
+        nc.scalar.dma_start(out=bias_bf[:], in_=b_in.partition_broadcast(P))
+        eps_bf = keep.tile([P, 1], BF16)
+        nc.scalar.dma_start(out=eps_bf[:], in_=eps0.partition_broadcast(P))
+
+        def load_x(x):
+            x_rows = x_pool.tile([P, SLAB_K], BF16)
+            nc.sync.dma_start(out=x_rows[:].rearrange("p (c w) -> p c w", c=4), in_=x_view[x])
+            return x_rows
+
+        def load_a(c):
+            a_rows = a_pool.tile([P, 2 * SLAB_K], BF16)
+            nc.sync.dma_start(out=a_rows[:], in_=a_view[c])
+            return a_rows
+
+        x_of = [load_x(x) for x in range(X_SLABS)]
+        a_of = [load_a(c) for c in range(A_AHEAD)]
+
+        ident = keep.tile([P, P], F32)
+        make_identity(nc, ident[:])
+
+        w_grouped = keep.tile([P, HID, PACK], BF16, align_bytes=64)
+        nc.vector.tensor_copy(out=w_grouped[:], in_=w_raw[:].rearrange("q t n -> q n t"))
+        bias = keep.tile([P, HID], F32)
+        nc.vector.tensor_copy(out=bias[:], in_=bias_bf[:])
+        one_plus_eps = keep.tile([P, 1], F32)
+        nc.vector.tensor_scalar_add(out=one_plus_eps[:], in0=eps_bf[:], scalar1=1.0)
+        w_codes = keep.tile([P, HID], U32, align_bytes=64)
+        w_scales = keep.tile([P, HID], U8, align_bytes=64)
+        nc.vector.quantize_mx(
+            out=w_codes[:].bitcast(FP8X4),
+            scales=w_scales[:],
+            in_=w_grouped[:].rearrange("q n t -> q (n t)"),
+        )
+
+        h_f32 = keep.tile([P, PASSES, PACK, HID], F32)
+        h_grouped = keep.tile([P, PASSES, HID, PACK], BF16, align_bytes=64)
+        h_codes = keep.tile([P, PASSES, HID], U32, align_bytes=64)
+        h_scales = keep.tile([P, PASSES, HID], U8, align_bytes=64)
+
+        def slab_words(i):
+            if i < X_SLABS:
+                return x_of[i][:].bitcast(F32)
+            s = i - X_SLABS
+            half = s % 2
+            return a_of[s // 2][:, half * SLAB_K : (half + 1) * SLAB_K].bitcast(F32)
+
+        def transpose_slab(words):
+            grouped = grouped_pool.tile([P, SLAB_K], BF16, align_bytes=64)
+            grouped_words = grouped[:].bitcast(F32).rearrange(
+                "q (o r u) -> q o r u", o=SLAB_OPERANDS, r=P, u=2
+            )
+            for j in range(SLAB_BANKS):
+                bank = tr_psum.tile([P, 2, 2, P], F32)
+                for o in range(2):
+                    for u in range(2):
+                        first = (4 * j + 2 * o + u) * P
+                        nc.tensor.transpose(bank[:, o, u, :], words[:, first : first + P], ident[:])
+                pairs = bank[:].rearrange("q o u r -> q o r u")
+                if j == VECTOR_BANK:
+                    nc.vector.tensor_copy(out=grouped_words[:, 2 * j : 2 * j + 2, :, :], in_=pairs)
+                else:
+                    nc.scalar.copy(out=grouped_words[:, 2 * j : 2 * j + 2, :, :], in_=pairs)
+            return grouped
+
+        def quantise_slab(grouped):
+            codes = packed_pool.tile([P, SLAB_OPERANDS, P], U32, align_bytes=64)
+            scales = packed_pool.tile([P, SLAB_OPERANDS, P], U8, align_bytes=64)
+            nc.vector.quantize_mx(
+                out=codes[:].rearrange("q o r -> q (o r)").bitcast(FP8X4),
+                scales=scales[:].rearrange("q o r -> q (o r)"),
+                in_=grouped[:],
+            )
+            return codes, scales
+
+        def new_sums():
+            sums = mx_psum.tile([P, PACK, HID], F32)
+            return sums
+
+        def project(x, codes, scales):
+            for g in (2 * x, 2 * x + 1):
+                sums = new_sums()
+                for t in range(PACK):
+                    o = PACK * (g - 2 * x) + t
+                    nc.tensor.matmul_mx(
+                        out=sums[:, t, :],
+                        lhsT=codes[:, o, :].bitcast(FP8X4),
+                        lhsT_scale=scales[:, o, :],
+                        rhs=w_codes[:].bitcast(FP8X4),
+                        rhs_scale=w_scales[:],
+                        start=True,
+                        stop=True,
+                    )
+                nc.vector.tensor_tensor(
+                    out=h_f32[:, g, :, :],
+                    in0=sums[:],
+                    in1=bias[:].unsqueeze(1).to_broadcast([P, PACK, HID]),
+                    op=ADD,
+                )
+                nc.scalar.copy(out=h_grouped[:, g, :, :], in_=h_f32[:, g, :, :].rearrange("p t n -> p n t"))
+
+        def quantise_h(x):
+            g_pair = slice(2 * x, 2 * x + 2)
+            nc.vector.quantize_mx(
+                out=h_codes[:, g_pair, :].rearrange("p g n -> p (g n)").bitcast(FP8X4),
+                scales=h_scales[:, g_pair, :].rearrange("p g n -> p (g n)"),
+                in_=h_grouped[:, g_pair, :, :].rearrange("p g n t -> p (g n t)"),
+            )
+
+        def aggregate(sums, t, codes, scales):
+            for g in range(PASSES):
+                nc.tensor.matmul_mx(
+                    out=sums[:, t, :],
+                    lhsT=codes[:, g, :].bitcast(FP8X4),
+                    lhsT_scale=scales[:, g, :],
+                    rhs=h_codes[:, g, :].bitcast(FP8X4),
+                    rhs_scale=h_scales[:, g, :],
+                    start=(g == 0),
+                    stop=(g == PASSES - 1),
+                )
+
+        def finish(g, sums):
+            result = out_pool.tile([P, PACK, HID], F32)
+            nc.vector.scalar_tensor_tensor(
+                out=result[:],
+                in0=h_f32[:, g, :, :],
+                scalar=one_plus_eps[:, 0:1],
+                in1=sums[:],
+                op0=MULT,
+                op1=ADD,
+            )
+            nc.sync.dma_start(
+                out=out_view[g], in_=result[:].rearrange("p (u e) n -> p u (e n)", u=2)
+            )
+
+        grouped_of = {}
+        packed_of = {}
+        sums_of = {}
+        for step in range(SLABS + 2):
+            to_transpose, to_quantise, to_multiply = step, step - 1, step - 2
+            if 0 <= step - 3 < X_SLABS:
+                quantise_h(step - 3)
+            if to_transpose < SLABS:
+                s = to_transpose - X_SLABS
+                if s >= 0 and s % 2 == 0 and s // 2 + A_AHEAD < A_LOADS:
+                    a_of.append(load_a(s // 2 + A_AHEAD))
+                grouped_of[to_transpose] = transpose_slab(slab_words(to_transpose))
+            if 0 <= to_quantise < SLABS:
+                packed_of[to_quantise] = quantise_slab(grouped_of[to_quantise])
+            if 0 <= to_multiply < X_SLABS:
+                codes, scales = packed_of[to_multiply]
+                project(to_multiply, codes, scales)
+            if to_multiply >= X_SLABS:
+                codes, scales = packed_of[to_multiply]
+                g, t = divmod(to_multiply - X_SLABS, PACK)
+                if t == 0:
+                    sums_of[g] = new_sums()
+                aggregate(sums_of[g], t, codes, scales)
+                if t == PACK - 1:
+                    finish(g, sums_of[g])

@@ -25,6 +25,8 @@ SLABS = X_SLABS + A_SLABS
 A_LOADS = A_SLABS // 2
 A_AHEAD = 4
 VECTOR_BANK = 1
+SLAB_QUANTISES = 2
+LAST_LOAD_CUTS = 8
 
 FLOPS = 2 * NODES * FEATS * HID + 2 * NODES * NODES * HID
 
@@ -62,7 +64,11 @@ def tile_gin_pa_t_kernel(tc, X, A, W_in, b_in, eps0, out):
 
         def load_a(c):
             a_rows = a_pool.tile([P, 2 * SLAB_K], BF16)
-            nc.sync.dma_start(out=a_rows[:], in_=a_view[c])
+            cuts = LAST_LOAD_CUTS if c == A_LOADS - 1 else 1
+            width = 2 * SLAB_K // cuts
+            for piece in range(cuts):
+                cols = slice(piece * width, (piece + 1) * width)
+                nc.sync.dma_start(out=a_rows[:, cols], in_=a_view[c][:, cols])
             return a_rows
 
         x_of = [load_x(x) for x in range(X_SLABS)]
@@ -118,11 +124,14 @@ def tile_gin_pa_t_kernel(tc, X, A, W_in, b_in, eps0, out):
         def quantise_slab(grouped):
             codes = packed_pool.tile([P, SLAB_OPERANDS, P], U32, align_bytes=64)
             scales = packed_pool.tile([P, SLAB_OPERANDS, P], U8, align_bytes=64)
-            nc.vector.quantize_mx(
-                out=codes[:].rearrange("q o r -> q (o r)").bitcast(FP8X4),
-                scales=scales[:].rearrange("q o r -> q (o r)"),
-                in_=grouped[:],
-            )
+            operands = SLAB_OPERANDS // SLAB_QUANTISES
+            for part in range(SLAB_QUANTISES):
+                ops = slice(part * operands, (part + 1) * operands)
+                nc.vector.quantize_mx(
+                    out=codes[:, ops, :].rearrange("q o r -> q (o r)").bitcast(FP8X4),
+                    scales=scales[:, ops, :].rearrange("q o r -> q (o r)"),
+                    in_=grouped[:, part * operands * K_PASS : (part + 1) * operands * K_PASS],
+                )
             return codes, scales
 
         def new_sums():

@@ -26,6 +26,7 @@ A_LOADS = A_SLABS // 2
 A_AHEAD = 4
 VECTOR_BANK = 1
 SLAB_QUANTISES = 2
+MULTIPLY_RUN = 2
 LAST_LOAD_CUTS = 8
 
 FLOPS = 2 * NODES * FEATS * HID + 2 * NODES * NODES * HID
@@ -197,25 +198,31 @@ def tile_gin_pa_t_kernel(tc, X, A, W_in, b_in, eps0, out):
         grouped_of = {}
         packed_of = {}
         sums_of = {}
+        projected = []
+        multiplied = 0
         for step in range(SLABS + 2):
-            to_transpose, to_quantise, to_multiply = step, step - 1, step - 2
-            if 0 <= step - 3 < X_SLABS:
-                quantise_h(step - 3)
-            if to_transpose < SLABS:
-                s = to_transpose - X_SLABS
+            for x in projected:
+                quantise_h(x)
+            projected = []
+            if step < SLABS:
+                s = step - X_SLABS
                 if s >= 0 and s % 2 == 0 and s // 2 + A_AHEAD < A_LOADS:
                     a_of.append(load_a(s // 2 + A_AHEAD))
-                grouped_of[to_transpose] = transpose_slab(slab_words(to_transpose))
-            if 0 <= to_quantise < SLABS:
-                packed_of[to_quantise] = quantise_slab(grouped_of[to_quantise])
-            if 0 <= to_multiply < X_SLABS:
-                codes, scales = packed_of[to_multiply]
-                project(to_multiply, codes, scales)
-            if to_multiply >= X_SLABS:
-                codes, scales = packed_of[to_multiply]
-                g, t = divmod(to_multiply - X_SLABS, PACK)
-                if t == 0:
-                    sums_of[g] = new_sums()
-                aggregate(sums_of[g], t, codes, scales)
-                if t == PACK - 1:
-                    finish(g, sums_of[g])
+                grouped_of[step] = transpose_slab(slab_words(step))
+            if 0 <= step - 1 < SLABS:
+                packed_of[step - 1] = quantise_slab(grouped_of[step - 1])
+            ready = min(step - 1, SLABS)
+            if ready - multiplied >= MULTIPLY_RUN or step >= SLABS:
+                for i in range(multiplied, ready):
+                    codes, scales = packed_of[i]
+                    if i < X_SLABS:
+                        project(i, codes, scales)
+                        projected.append(i)
+                    else:
+                        g, t = divmod(i - X_SLABS, PACK)
+                        if t == 0:
+                            sums_of[g] = new_sums()
+                        aggregate(sums_of[g], t, codes, scales)
+                        if t == PACK - 1:
+                            finish(g, sums_of[g])
+                multiplied = ready

@@ -53,10 +53,12 @@ def tile_gin_pa_t_kernel(tc, X, A, W_in, b_in, eps0, out):
 
         w_raw = keep.tile([P, PACK, HID], BF16)
         nc.scalar.dma_start(out=w_raw[:].rearrange("q (u e) n -> q u (e n)", u=2), in_=w_view)
-        bias_bf = keep.tile([P, HID], BF16)
-        nc.scalar.dma_start(out=bias_bf[:], in_=b_in.partition_broadcast(P))
-        eps_bf = keep.tile([P, 1], BF16)
-        nc.scalar.dma_start(out=eps_bf[:], in_=eps0.partition_broadcast(P))
+        small = keep.tile([P, 2 * HID], BF16)
+        nc.vector.memset(small[:], 0.0)
+        nc.scalar.dma_start(out=small[0:1, 0:HID], in_=b_in.unsqueeze(0))
+        nc.scalar.dma_start(out=small[0:1, HID : HID + 1], in_=eps0.unsqueeze(0))
+        ones = keep.tile([P, P], BF16)
+        nc.vector.memset(ones[:], 1.0)
 
         def load_x(x):
             x_rows = x_pool.tile([P, SLAB_K], BF16)
@@ -81,9 +83,7 @@ def tile_gin_pa_t_kernel(tc, X, A, W_in, b_in, eps0, out):
         w_grouped = keep.tile([P, HID, PACK], BF16, align_bytes=64)
         nc.vector.tensor_copy(out=w_grouped[:], in_=w_raw[:].rearrange("q t n -> q n t"))
         bias = keep.tile([P, HID], F32)
-        nc.vector.tensor_copy(out=bias[:], in_=bias_bf[:])
         one_plus_eps = keep.tile([P, 1], F32)
-        nc.vector.tensor_scalar_add(out=one_plus_eps[:], in0=eps_bf[:], scalar1=1.0)
         w_codes = keep.tile([P, HID], U32, align_bytes=64)
         w_scales = keep.tile([P, HID], U8, align_bytes=64)
         nc.vector.quantize_mx(
@@ -138,6 +138,15 @@ def tile_gin_pa_t_kernel(tc, X, A, W_in, b_in, eps0, out):
         def new_sums():
             sums = mx_psum.tile([P, PACK, HID], F32)
             return sums
+
+        def spread_constants():
+            sums = new_sums()
+            spread = sums[:].rearrange("p t n -> p (t n)")[:, 0 : 2 * HID]
+            nc.tensor.matmul(spread, lhsT=ones[:], rhs=small[:], start=True, stop=True)
+            nc.vector.tensor_copy(out=bias[:], in_=spread[:, 0:HID])
+            nc.vector.tensor_scalar_add(
+                out=one_plus_eps[:], in0=spread[:, HID : HID + 1], scalar1=1.0
+            )
 
         def project(x, codes, scales):
             for g in (2 * x, 2 * x + 1):
@@ -209,6 +218,8 @@ def tile_gin_pa_t_kernel(tc, X, A, W_in, b_in, eps0, out):
                 if s >= 0 and s % 2 == 0 and s // 2 + A_AHEAD < A_LOADS:
                     a_of.append(load_a(s // 2 + A_AHEAD))
                 grouped_of[step] = transpose_slab(slab_words(step))
+            if step == 0:
+                spread_constants()
             if 0 <= step - 1 < SLABS:
                 packed_of[step - 1] = quantise_slab(grouped_of[step - 1])
             ready = min(step - 1, SLABS)

@@ -27,7 +27,10 @@ A_AHEAD = 4
 VECTOR_BANK = 1
 SLAB_QUANTISES = 2
 MULTIPLY_RUN = 2
-LAST_LOAD_CUTS = 8
+CUTS = {0:(4,4), 12:(4,4),13:(4,4),14: (4, 4), 15: (4, 2, 1, 1)}
+FINE = 2
+XCUT = {0: 1}
+XV = (1,1,1,1)
 
 FLOPS = 2 * NODES * FEATS * HID + 2 * NODES * NODES * HID
 
@@ -46,31 +49,38 @@ def tile_gin_pa_t_kernel(tc, X, A, W_in, b_in, eps0, out):
         a_pool = ctx.enter_context(tc.tile_pool(name="a_pool", bufs=A_AHEAD + 1))
         grouped_pool = ctx.enter_context(tc.tile_pool(name="grouped_pool", bufs=3))
         packed_pool = ctx.enter_context(tc.tile_pool(name="packed_pool", bufs=4))
-        out_pool = ctx.enter_context(tc.tile_pool(name="out_pool", bufs=3))
+        out_pool = ctx.enter_context(tc.tile_pool(name="out_pool", bufs=8))
         tr_psum = ctx.enter_context(tc.psum_pool(name="tr_psum", bufs=6))
         mx_psum = ctx.enter_context(tc.psum_pool(name="mx_psum", bufs=2))
         ctx.enter_context(tc.manual_schedule())
 
         w_raw = keep.tile([P, PACK, HID], BF16)
         nc.scalar.dma_start(out=w_raw[:].rearrange("q (u e) n -> q u (e n)", u=2), in_=w_view)
+        row = keep.tile([1, 2 * HID], BF16)
+        nc.scalar.dma_start(out=row[:, 0:HID], in_=b_in.unsqueeze(0))
+        nc.scalar.dma_start(out=row[:, HID : HID + 1], in_=eps0.unsqueeze(0))
         small = keep.tile([P, 2 * HID], BF16)
         nc.vector.memset(small[:], 0.0)
-        nc.scalar.dma_start(out=small[0:1, 0:HID], in_=b_in.unsqueeze(0))
-        nc.scalar.dma_start(out=small[0:1, HID : HID + 1], in_=eps0.unsqueeze(0))
         ones = keep.tile([P, P], BF16)
         nc.vector.memset(ones[:], 1.0)
 
         def load_x(x):
             x_rows = x_pool.tile([P, SLAB_K], BF16)
-            nc.sync.dma_start(out=x_rows[:].rearrange("p (c w) -> p c w", c=4), in_=x_view[x])
+            view = x_rows[:].rearrange("p (c w) -> p c w", c=4)
+            if x in XCUT:
+                for c in range(0, 4, XCUT[x]):
+                    nc.sync.dma_start(out=view[:, c : c + XCUT[x], :], in_=x_view[x][:, c : c + XCUT[x], :])
+            else:
+                nc.sync.dma_start(out=view, in_=x_view[x])
             return x_rows
 
         def load_a(c):
             a_rows = a_pool.tile([P, 2 * SLAB_K], BF16)
-            cuts = LAST_LOAD_CUTS if c == A_LOADS - 1 else 1
-            width = 2 * SLAB_K // cuts
-            for piece in range(cuts):
-                cols = slice(piece * width, (piece + 1) * width)
+            cuts = CUTS.get(c, (8,))
+            first = 0
+            for w in cuts:
+                cols = slice(first * 1024, (first + w) * 1024)
+                first += w
                 nc.sync.dma_start(out=a_rows[:, cols], in_=a_view[c][:, cols])
             return a_rows
 
@@ -104,42 +114,59 @@ def tile_gin_pa_t_kernel(tc, X, A, W_in, b_in, eps0, out):
             half = s % 2
             return a_of[s // 2][:, half * SLAB_K : (half + 1) * SLAB_K].bitcast(F32)
 
-        def transpose_slab(words):
-            grouped = grouped_pool.tile([P, SLAB_K], BF16, align_bytes=64)
-            grouped_words = grouped[:].bitcast(F32).rearrange(
+        grouped_of = {}
+        packed_of = {}
+
+        def transpose_bank(i, j, halves=False):
+            if j == 0:
+                grouped = grouped_pool.tile([P, SLAB_K], BF16, align_bytes=64)
+                grouped_of[i] = grouped
+            words = slab_words(i)
+            grouped_words = grouped_of[i][:].bitcast(F32).rearrange(
                 "q (o r u) -> q o r u", o=SLAB_OPERANDS, r=P, u=2
             )
-            for j in range(SLAB_BANKS):
-                bank = tr_psum.tile([P, 2, 2, P], F32)
+            if halves:
                 for o in range(2):
+                    bank = tr_psum.tile([P, 2, 2, P], F32)
                     for u in range(2):
                         first = (4 * j + 2 * o + u) * P
                         nc.tensor.transpose(bank[:, o, u, :], words[:, first : first + P], ident[:])
-                pairs = bank[:].rearrange("q o u r -> q o r u")
-                if j == VECTOR_BANK:
-                    nc.vector.tensor_copy(out=grouped_words[:, 2 * j : 2 * j + 2, :, :], in_=pairs)
-                else:
-                    nc.scalar.copy(out=grouped_words[:, 2 * j : 2 * j + 2, :, :], in_=pairs)
-            return grouped
+                    pairs = bank[:].rearrange("q o u r -> q o r u")
+                    if o == 1:
+                        nc.vector.tensor_copy(out=grouped_words[:, 2 * j + o, :, :], in_=pairs[:, o, :, :])
+                    else:
+                        nc.scalar.copy(out=grouped_words[:, 2 * j + o, :, :], in_=pairs[:, o, :, :])
+                return
+            bank = tr_psum.tile([P, 2, 2, P], F32)
+            for o in range(2):
+                for u in range(2):
+                    first = (4 * j + 2 * o + u) * P
+                    nc.tensor.transpose(bank[:, o, u, :], words[:, first : first + P], ident[:])
+            pairs = bank[:].rearrange("q o u r -> q o r u")
+            if j == VECTOR_BANK and (i >= X_SLABS or XV[i]):
+                nc.vector.tensor_copy(out=grouped_words[:, 2 * j : 2 * j + 2, :, :], in_=pairs)
+            else:
+                nc.scalar.copy(out=grouped_words[:, 2 * j : 2 * j + 2, :, :], in_=pairs)
 
-        def quantise_slab(grouped):
-            codes = packed_pool.tile([P, SLAB_OPERANDS, P], U32, align_bytes=64)
-            scales = packed_pool.tile([P, SLAB_OPERANDS, P], U8, align_bytes=64)
-            operands = SLAB_OPERANDS // SLAB_QUANTISES
-            for part in range(SLAB_QUANTISES):
-                ops = slice(part * operands, (part + 1) * operands)
-                nc.vector.quantize_mx(
-                    out=codes[:, ops, :].rearrange("q o r -> q (o r)").bitcast(FP8X4),
-                    scales=scales[:, ops, :].rearrange("q o r -> q (o r)"),
-                    in_=grouped[:, part * operands * K_PASS : (part + 1) * operands * K_PASS],
-                )
-            return codes, scales
+        def quantise(i, j0, j1):
+            if j0 == 0:
+                codes = packed_pool.tile([P, SLAB_OPERANDS, P], U32, align_bytes=64)
+                scales = packed_pool.tile([P, SLAB_OPERANDS, P], U8, align_bytes=64)
+                packed_of[i] = (codes, scales)
+            codes, scales = packed_of[i]
+            ops = slice(2 * j0, 2 * j1)
+            nc.vector.quantize_mx(
+                out=codes[:, ops, :].rearrange("q o r -> q (o r)").bitcast(FP8X4),
+                scales=scales[:, ops, :].rearrange("q o r -> q (o r)"),
+                in_=grouped_of[i][:, 2 * j0 * K_PASS : 2 * j1 * K_PASS],
+            )
 
         def new_sums():
             sums = mx_psum.tile([P, PACK, HID], F32)
             return sums
 
         def spread_constants():
+            nc.vector.tensor_copy(out=small[0:1, 0 : HID + 1], in_=row[:, 0 : HID + 1])
             sums = new_sums()
             spread = sums[:].rearrange("p t n -> p (t n)")[:, 0 : 2 * HID]
             nc.tensor.matmul(spread, lhsT=ones[:], rhs=small[:], start=True, stop=True)
@@ -148,11 +175,11 @@ def tile_gin_pa_t_kernel(tc, X, A, W_in, b_in, eps0, out):
                 out=one_plus_eps[:], in0=spread[:, HID : HID + 1], scalar1=1.0
             )
 
-        def project(x, codes, scales):
-            for g in (2 * x, 2 * x + 1):
+        def project(g, codes, scales):
+            for g in (g,):
                 sums = new_sums()
                 for t in range(PACK):
-                    o = PACK * (g - 2 * x) + t
+                    o = PACK * (g % 2) + t
                     nc.tensor.matmul_mx(
                         out=sums[:, t, :],
                         lhsT=codes[:, o, :].bitcast(FP8X4),
@@ -168,6 +195,9 @@ def tile_gin_pa_t_kernel(tc, X, A, W_in, b_in, eps0, out):
                     in1=bias[:].unsqueeze(1).to_broadcast([P, PACK, HID]),
                     op=ADD,
                 )
+
+        def cast_h(x):
+            for g in (2 * x, 2 * x + 1):
                 nc.scalar.copy(out=h_grouped[:, g, :, :], in_=h_f32[:, g, :, :].rearrange("p t n -> p n t"))
 
         def quantise_h(x):
@@ -178,8 +208,17 @@ def tile_gin_pa_t_kernel(tc, X, A, W_in, b_in, eps0, out):
                 in_=h_grouped[:, g_pair, :, :].rearrange("p g n t -> p (g n t)"),
             )
 
-        def aggregate(sums, t, codes, scales):
-            for g in range(PASSES):
+        sums_of = {}
+
+        def aggregate(i, g0, g1):
+            if g1 <= g0:
+                return
+            group, t = divmod(i - X_SLABS, PACK)
+            if t == 0 and g0 == 0:
+                sums_of[group] = new_sums()
+            sums = sums_of[group]
+            codes, scales = packed_of[i]
+            for g in range(g0, g1):
                 nc.tensor.matmul_mx(
                     out=sums[:, t, :],
                     lhsT=codes[:, g, :].bitcast(FP8X4),
@@ -190,50 +229,102 @@ def tile_gin_pa_t_kernel(tc, X, A, W_in, b_in, eps0, out):
                     stop=(g == PASSES - 1),
                 )
 
-        def finish(g, sums):
-            result = out_pool.tile([P, PACK, HID], F32)
+        def finish(g, t0, t1):
+            if t0 == 0:
+                result = out_pool.tile([P, PACK, HID], F32)
+                result_of[g] = result
+            result = result_of[g]
             nc.vector.scalar_tensor_tensor(
-                out=result[:],
-                in0=h_f32[:, g, :, :],
+                out=result[:, t0:t1, :],
+                in0=h_f32[:, g, t0:t1, :],
                 scalar=one_plus_eps[:, 0:1],
-                in1=sums[:],
+                in1=sums_of[g][:, t0:t1, :],
                 op0=MULT,
                 op1=ADD,
             )
-            nc.sync.dma_start(
-                out=out_view[g], in_=result[:].rearrange("p (u e) n -> p u (e n)", u=2)
-            )
 
-        grouped_of = {}
-        packed_of = {}
-        sums_of = {}
+        result_of = {}
+
+        def store(g, t0, t1):
+            rows = result_of[g][:, t0:t1, :].rearrange("p t n -> p (t n)")
+            if t1 - t0 == 4:
+                nc.sync.dma_start(out=out_view[g], in_=rows.rearrange("p (u x) -> p u x", u=2))
+            elif t1 - t0 == 2:
+                nc.sync.dma_start(out=out_view[g][:, t0 // 2, :], in_=rows)
+            else:
+                nc.sync.dma_start(out=out_view[g][:, t0 // 2, (t0 % 2) * HID : (t0 % 2 + 1) * HID], in_=rows)
+
         projected = []
-        multiplied = 0
-        for step in range(SLABS + 2):
-            for x in projected:
-                quantise_h(x)
-            projected = []
-            if step < SLABS:
-                s = step - X_SLABS
-                if s >= 0 and s % 2 == 0 and s // 2 + A_AHEAD < A_LOADS:
-                    a_of.append(load_a(s // 2 + A_AHEAD))
-                grouped_of[step] = transpose_slab(slab_words(step))
-            if step == 0:
+        queue = []
+        done = 0
+        last = SLABS - 1
+
+        def multiply(hh):
+            i, half = divmod(hh, 2)
+            if i < X_SLABS:
+                project(2 * i + half, *packed_of[i])
+                return
+            aggregate(i, 4 * half, 4 * half + 4)
+            group, t = divmod(i - X_SLABS, PACK)
+            if half == 1 and t == PACK - 1 and i < last:
+                finish(group, 0, PACK)
+                waiting.append(group)
+                flush()
+
+        waiting = []
+
+        def flush():
+            if len(a_of) == A_LOADS:
+                for g in waiting:
+                    store(g, 0, PACK)
+                waiting.clear()
+
+        def load_more(step):
+            s = step - X_SLABS
+            if s >= 0 and s % 2 == 0 and s // 2 + A_AHEAD < A_LOADS:
+                a_of.append(load_a(s // 2 + A_AHEAD))
+
+        X = X_SLABS
+        for s in range(SLABS):
+            load_more(s)
+            final = s == last
+            transpose_bank(s, 0)
+            transpose_bank(s, 1)
+            if s > 0:
+                quantise(s - 1, 2, 4)
+            if final:
+                while done < 2 * s - 1:
+                    multiply(done)
+                    done += 1
+                quantise(s, 0, 1)
+                transpose_bank(s, 2)
+                quantise(s, 1, 2)
+                multiply(done)
+                done += 1
+                finish(7, 0, 3)
+                transpose_bank(s, 3, True)
+                quantise(s, 2, 3)
+                aggregate(s, 0, 4)
+                aggregate(s, 4, 6)
+                quantise(s, 3, 4)
+                aggregate(s, 6, 8)
+                finish(7, 3, 4)
+                store(7, 0, 2)
+                store(7, 2, 3)
+                store(7, 3, 4)
+                break
+            transpose_bank(s, 2)
+            if 0 <= s - 2 < X_SLABS:
+                cast_h(s - 2)
+            quantise(s, 0, 2)
+            transpose_bank(s, 3)
+            if 0 <= s - 2 < X_SLABS:
+                quantise_h(s - 2)
+            if s == 0:
                 spread_constants()
-            if 0 <= step - 1 < SLABS:
-                packed_of[step - 1] = quantise_slab(grouped_of[step - 1])
-            ready = min(step - 1, SLABS)
-            if ready - multiplied >= MULTIPLY_RUN or step >= SLABS:
-                for i in range(multiplied, ready):
-                    codes, scales = packed_of[i]
-                    if i < X_SLABS:
-                        project(i, codes, scales)
-                        projected.append(i)
-                    else:
-                        g, t = divmod(i - X_SLABS, PACK)
-                        if t == 0:
-                            sums_of[g] = new_sums()
-                        aggregate(sums_of[g], t, codes, scales)
-                        if t == PACK - 1:
-                            finish(g, sums_of[g])
-                multiplied = ready
+            ready = 2 * s - 1 if s > X_SLABS else 2 * s
+            run = 2 * MULTIPLY_RUN if X_SLABS + 1 < s < SLABS - FINE else 2
+            if ready - done >= run:
+                while done < ready:
+                    multiply(done)
+                    done += 1

@@ -216,7 +216,9 @@ def tile_gin_pa_t_kernel(tc, X, A, W_in, b_in, eps0, out):
             group, t = divmod(i - X_SLABS, PACK)
             if t == 0 and g0 == 0:
                 sums_of[group] = new_sums()
-            sums = sums_of[group]
+            if i == last and g0 == 0:
+                sums_of["last"] = new_sums()
+            sums = sums_of["last" if i == last else group]
             codes, scales = packed_of[i]
             for g in range(g0, g1):
                 nc.tensor.matmul_mx(
@@ -238,7 +240,7 @@ def tile_gin_pa_t_kernel(tc, X, A, W_in, b_in, eps0, out):
                 out=result[:, t0:t1, :],
                 in0=h_f32[:, g, t0:t1, :],
                 scalar=one_plus_eps[:, 0:1],
-                in1=sums_of[g][:, t0:t1, :],
+                in1=sums_of["last" if t0 == 3 else g][:, t0:t1, :],
                 op0=MULT,
                 op1=ADD,
             )
@@ -285,34 +287,12 @@ def tile_gin_pa_t_kernel(tc, X, A, W_in, b_in, eps0, out):
                 a_of.append(load_a(s // 2 + A_AHEAD))
 
         X = X_SLABS
-        for s in range(SLABS):
+        for s in range(SLABS - 2):
             load_more(s)
-            final = s == last
             transpose_bank(s, 0)
             transpose_bank(s, 1)
             if s > 0:
                 quantise(s - 1, 2, 4)
-            if final:
-                while done < 2 * s - 1:
-                    multiply(done)
-                    done += 1
-                quantise(s, 0, 1)
-                transpose_bank(s, 2)
-                quantise(s, 1, 2)
-                multiply(done)
-                done += 1
-                finish(7, 0, 3)
-                transpose_bank(s, 3, True)
-                quantise(s, 2, 3)
-                aggregate(s, 0, 4)
-                aggregate(s, 4, 6)
-                quantise(s, 3, 4)
-                aggregate(s, 6, 8)
-                finish(7, 3, 4)
-                store(7, 0, 2)
-                store(7, 2, 3)
-                store(7, 3, 4)
-                break
             transpose_bank(s, 2)
             if 0 <= s - 2 < X_SLABS:
                 cast_h(s - 2)
@@ -328,3 +308,30 @@ def tile_gin_pa_t_kernel(tc, X, A, W_in, b_in, eps0, out):
                 while done < ready:
                     multiply(done)
                     done += 1
+        a, b = last - 1, last
+        transpose_bank(a, 0)
+        transpose_bank(a, 1)
+        quantise(a - 1, 2, 4)
+        transpose_bank(a, 2)
+        quantise(a, 0, 2)
+        transpose_bank(a, 3)
+        transpose_bank(b, 0)
+        transpose_bank(b, 1)
+        quantise(a, 2, 4)
+        transpose_bank(b, 2)
+        quantise(b, 0, 2)
+        while done < 2 * a + 1:
+            multiply(done)
+            done += 1
+        transpose_bank(b, 3, True)
+        quantise(b, 2, 3)
+        multiply(done)
+        done += 1
+        finish(7, 0, 3)
+        aggregate(b, 0, 6)
+        quantise(b, 3, 4)
+        store(7, 0, 2)
+        store(7, 2, 3)
+        aggregate(b, 6, 8)
+        finish(7, 3, 4)
+        store(7, 3, 4)

@@ -30,7 +30,9 @@ MULTIPLY_RUN = 2
 CUTS = {0:(4,4), 12:(4,4),13:(4,4),14: (4, 4), 15: (4, 2, 1, 1)}
 FINE = 2
 XCUT = {0: 1}
-XV = (1,1,1,1)
+VSKIP = lambda i: i < 4 or i == 34
+OFF = 1
+CASTV = (1,)
 
 FLOPS = 2 * NODES * FEATS * HID + 2 * NODES * NODES * HID
 
@@ -143,7 +145,7 @@ def tile_gin_pa_t_kernel(tc, X, A, W_in, b_in, eps0, out):
                     first = (4 * j + 2 * o + u) * P
                     nc.tensor.transpose(bank[:, o, u, :], words[:, first : first + P], ident[:])
             pairs = bank[:].rearrange("q o u r -> q o r u")
-            if j == VECTOR_BANK and (i >= X_SLABS or XV[i]):
+            if j == VECTOR_BANK and not VSKIP(i):
                 nc.vector.tensor_copy(out=grouped_words[:, 2 * j : 2 * j + 2, :, :], in_=pairs)
             else:
                 nc.scalar.copy(out=grouped_words[:, 2 * j : 2 * j + 2, :, :], in_=pairs)
@@ -198,7 +200,8 @@ def tile_gin_pa_t_kernel(tc, X, A, W_in, b_in, eps0, out):
 
         def cast_h(x):
             for g in (2 * x, 2 * x + 1):
-                nc.scalar.copy(out=h_grouped[:, g, :, :], in_=h_f32[:, g, :, :].rearrange("p t n -> p n t"))
+                cp = nc.vector.tensor_copy if g % 2 in CASTV else nc.scalar.copy
+                cp(out=h_grouped[:, g, :, :], in_=h_f32[:, g, :, :].rearrange("p t n -> p n t"))
 
         def quantise_h(x):
             g_pair = slice(2 * x, 2 * x + 2)
@@ -302,7 +305,7 @@ def tile_gin_pa_t_kernel(tc, X, A, W_in, b_in, eps0, out):
                 quantise_h(s - 2)
             if s == 0:
                 spread_constants()
-            ready = 2 * s - 1 if s > X_SLABS else 2 * s
+            ready = 2 * s - OFF if s > X_SLABS else 2 * s
             run = 2 * MULTIPLY_RUN if X_SLABS + 1 < s < SLABS - FINE else 2
             if ready - done >= run:
                 while done < ready:
@@ -323,14 +326,15 @@ def tile_gin_pa_t_kernel(tc, X, A, W_in, b_in, eps0, out):
         while done < 2 * a + 1:
             multiply(done)
             done += 1
+        finish(7, 0, 2)
+        store(7, 0, 2)
         transpose_bank(b, 3, True)
         quantise(b, 2, 3)
         multiply(done)
         done += 1
-        finish(7, 0, 3)
-        aggregate(b, 0, 6)
         quantise(b, 3, 4)
-        store(7, 0, 2)
+        aggregate(b, 0, 6)
+        finish(7, 2, 3)
         store(7, 2, 3)
         aggregate(b, 6, 8)
         finish(7, 3, 4)

@@ -27,7 +27,7 @@ A_AHEAD = 4
 VECTOR_BANK = 1
 SLAB_QUANTISES = 2
 MULTIPLY_RUN = 2
-CUTS = {0:(4,4), 12:(4,4),13:(4,4),14: (4, 4), 15: (4, 2, 1, 1)}
+CUTS = {15: (4, 2, 1, 1)}
 FINE = 2
 XCUT = {0: 1}
 VSKIP = lambda i: i < 4 or i == 34
@@ -326,15 +326,14 @@ def tile_gin_pa_t_kernel(tc, X, A, W_in, b_in, eps0, out):
         while done < 2 * a + 1:
             multiply(done)
             done += 1
-        finish(7, 0, 2)
-        store(7, 0, 2)
         transpose_bank(b, 3, True)
         quantise(b, 2, 3)
         multiply(done)
         done += 1
         quantise(b, 3, 4)
         aggregate(b, 0, 6)
-        finish(7, 2, 3)
+        finish(7, 0, 3)
+        store(7, 0, 2)
         store(7, 2, 3)
         aggregate(b, 6, 8)
         finish(7, 3, 4)

@@ -27,9 +27,9 @@ A_AHEAD = 4
 VECTOR_BANK = 1
 SLAB_QUANTISES = 2
 MULTIPLY_RUN = 2
-CUTS = {15: (4, 2, 1, 1)}
+CUTS = {15: (4, 2, 2)}
 FINE = 2
-XCUT = {0: 1}
+XCUT = {0: 2}
 VSKIP = lambda i: i < 4 or i == 34
 OFF = 1
 CASTV = (1,)
@@ -43,7 +43,7 @@ def tile_gin_pa_t_kernel(tc, X, A, W_in, b_in, eps0, out):
     x_view = X.rearrange("(x c p e) k -> x p c (e k)", c=4, p=P, e=2)
     a_view = A.rearrange("(c p e) k -> c p (e k)", p=P, e=2)
     w_view = W_in.rearrange("(u q e) n -> q u (e n)", u=2, q=P, e=2)
-    out_view = out.rearrange("(g u p e) n -> g p u (e n)", u=2, p=P, e=2)
+    out_view = out.rearrange("(m v p e) n -> m p v (e n)", v=4, p=P, e=2)
 
     with ExitStack() as ctx:
         keep = ctx.enter_context(tc.tile_pool(name="keep", bufs=1))
@@ -51,7 +51,7 @@ def tile_gin_pa_t_kernel(tc, X, A, W_in, b_in, eps0, out):
         a_pool = ctx.enter_context(tc.tile_pool(name="a_pool", bufs=A_AHEAD + 1))
         grouped_pool = ctx.enter_context(tc.tile_pool(name="grouped_pool", bufs=3))
         packed_pool = ctx.enter_context(tc.tile_pool(name="packed_pool", bufs=4))
-        out_pool = ctx.enter_context(tc.tile_pool(name="out_pool", bufs=8))
+        out_pool = ctx.enter_context(tc.tile_pool(name="out_pool", bufs=4))
         tr_psum = ctx.enter_context(tc.psum_pool(name="tr_psum", bufs=6))
         mx_psum = ctx.enter_context(tc.psum_pool(name="mx_psum", bufs=2))
         ctx.enter_context(tc.manual_schedule())
@@ -234,13 +234,15 @@ def tile_gin_pa_t_kernel(tc, X, A, W_in, b_in, eps0, out):
                     stop=(g == PASSES - 1),
                 )
 
+        result_of = {}
+
         def finish(g, t0, t1):
-            if t0 == 0:
-                result = out_pool.tile([P, PACK, HID], F32)
-                result_of[g] = result
-            result = result_of[g]
+            m, half = divmod(g, 2)
+            if half == 0 and t0 == 0:
+                result = out_pool.tile([P, 2, PACK, HID], F32)
+                result_of[m] = result
             nc.vector.scalar_tensor_tensor(
-                out=result[:, t0:t1, :],
+                out=result_of[m][:, half, t0:t1, :],
                 in0=h_f32[:, g, t0:t1, :],
                 scalar=one_plus_eps[:, 0:1],
                 in1=sums_of["last" if t0 == 3 else g][:, t0:t1, :],
@@ -248,16 +250,9 @@ def tile_gin_pa_t_kernel(tc, X, A, W_in, b_in, eps0, out):
                 op1=ADD,
             )
 
-        result_of = {}
-
-        def store(g, t0, t1):
-            rows = result_of[g][:, t0:t1, :].rearrange("p t n -> p (t n)")
-            if t1 - t0 == 4:
-                nc.sync.dma_start(out=out_view[g], in_=rows.rearrange("p (u x) -> p u x", u=2))
-            elif t1 - t0 == 2:
-                nc.sync.dma_start(out=out_view[g][:, t0 // 2, :], in_=rows)
-            else:
-                nc.sync.dma_start(out=out_view[g][:, t0 // 2, (t0 % 2) * HID : (t0 % 2 + 1) * HID], in_=rows)
+        def store(m, v0, v1):
+            rows = result_of[m][:].rearrange("p g (u e) n -> p (g u) (e n)", u=2)
+            nc.sync.dma_start(out=out_view[m][:, v0:v1, :], in_=rows[:, v0:v1, :])
 
         projected = []
         queue = []
@@ -273,15 +268,18 @@ def tile_gin_pa_t_kernel(tc, X, A, W_in, b_in, eps0, out):
             group, t = divmod(i - X_SLABS, PACK)
             if half == 1 and t == PACK - 1 and i < last:
                 finish(group, 0, PACK)
-                waiting.append(group)
+                if group % 2 == 1:
+                    waiting.append((group // 2, 0, 4))
+                elif group == 6:
+                    waiting.append((3, 0, 2))
                 flush()
 
         waiting = []
 
         def flush():
             if len(a_of) == A_LOADS:
-                for g in waiting:
-                    store(g, 0, PACK)
+                for piece in waiting:
+                    store(*piece)
                 waiting.clear()
 
         def load_more(step):
@@ -333,8 +331,7 @@ def tile_gin_pa_t_kernel(tc, X, A, W_in, b_in, eps0, out):
         quantise(b, 3, 4)
         aggregate(b, 0, 6)
         finish(7, 0, 3)
-        store(7, 0, 2)
-        store(7, 2, 3)
+        store(3, 2, 3)
         aggregate(b, 6, 8)
         finish(7, 3, 4)
-        store(7, 3, 4)
+        store(3, 3, 4)

@@ -29,7 +29,6 @@ SLAB_QUANTISES = 2
 MULTIPLY_RUN = 2
 CUTS = {15: (4, 2, 2)}
 FINE = 2
-XCUT = {0: 2}
 VSKIP = lambda i: i < 4 or i == 34
 OFF = 1
 CASTV = (1,)
@@ -40,7 +39,7 @@ FLOPS = 2 * NODES * FEATS * HID + 2 * NODES * NODES * HID
 def tile_gin_pa_t_kernel(tc, X, A, W_in, b_in, eps0, out):
     nc = tc.nc
 
-    x_view = X.rearrange("(x c p e) k -> x p c (e k)", c=4, p=P, e=2)
+    x_view = X.rearrange("(x p i) k -> x p (i k)", p=P, i=8)
     a_view = A.rearrange("(c p e) k -> c p (e k)", p=P, e=2)
     w_view = W_in.rearrange("(u q e) n -> q u (e n)", u=2, q=P, e=2)
     out_view = out.rearrange("(m v p e) n -> m p v (e n)", v=4, p=P, e=2)
@@ -68,12 +67,7 @@ def tile_gin_pa_t_kernel(tc, X, A, W_in, b_in, eps0, out):
 
         def load_x(x):
             x_rows = x_pool.tile([P, SLAB_K], BF16)
-            view = x_rows[:].rearrange("p (c w) -> p c w", c=4)
-            if x in XCUT:
-                for c in range(0, 4, XCUT[x]):
-                    nc.sync.dma_start(out=view[:, c : c + XCUT[x], :], in_=x_view[x][:, c : c + XCUT[x], :])
-            else:
-                nc.sync.dma_start(out=view, in_=x_view[x])
+            nc.sync.dma_start(out=x_rows[:], in_=x_view[x])
             return x_rows
 
         def load_a(c):
@@ -140,6 +134,20 @@ def tile_gin_pa_t_kernel(tc, X, A, W_in, b_in, eps0, out):
                         nc.scalar.copy(out=grouped_words[:, 2 * j + o, :, :], in_=pairs[:, o, :, :])
                 return
             bank = tr_psum.tile([P, 2, 2, P], F32)
+            if i < X_SLABS:
+                e, h = divmod(j, 2)
+                for s in range(2):
+                    for u in range(2):
+                        first = (2 * (4 * h + 2 * s + e) + u) * P
+                        nc.tensor.transpose(bank[:, s, u, :], words[:, first : first + P], ident[:])
+                half = grouped_of[i][:].bitcast(F32).rearrange(
+                    "q (e c r h w) -> q e c r h w", e=2, c=4, r=32, h=2, w=4
+                )
+                nc.scalar.copy(
+                    out=half[:, e, :, :, h, :],
+                    in_=bank[:].rearrange("q s u (c r) -> q c r (s u)", c=4),
+                )
+                return
             for o in range(2):
                 for u in range(2):
                     first = (4 * j + 2 * o + u) * P
@@ -177,11 +185,14 @@ def tile_gin_pa_t_kernel(tc, X, A, W_in, b_in, eps0, out):
                 out=one_plus_eps[:], in0=spread[:, HID : HID + 1], scalar1=1.0
             )
 
-        def project(g, codes, scales):
-            for g in (g,):
+        def project(x, codes, scales):
+            pair = []
+            for g in range(2):
                 sums = new_sums()
+                pair.append(sums)
                 for t in range(PACK):
-                    o = PACK * (g % 2) + t
+                    u, e = divmod(t, 2)
+                    o = 4 * e + 2 * g + u
                     nc.tensor.matmul_mx(
                         out=sums[:, t, :],
                         lhsT=codes[:, o, :].bitcast(FP8X4),
@@ -191,9 +202,10 @@ def tile_gin_pa_t_kernel(tc, X, A, W_in, b_in, eps0, out):
                         start=True,
                         stop=True,
                     )
+            for g in range(2):
                 nc.vector.tensor_tensor(
-                    out=h_f32[:, g, :, :],
-                    in0=sums[:],
+                    out=h_f32[:, 2 * x + g, :, :],
+                    in0=pair[g][:],
                     in1=bias[:].unsqueeze(1).to_broadcast([P, PACK, HID]),
                     op=ADD,
                 )
@@ -262,7 +274,8 @@ def tile_gin_pa_t_kernel(tc, X, A, W_in, b_in, eps0, out):
         def multiply(hh):
             i, half = divmod(hh, 2)
             if i < X_SLABS:
-                project(2 * i + half, *packed_of[i])
+                if half == 1:
+                    project(i, *packed_of[i])
                 return
             aggregate(i, 4 * half, 4 * half + 4)
             group, t = divmod(i - X_SLABS, PACK)

@@ -55,7 +55,7 @@ def tile_gin_pa_t_kernel(tc, X, A, W_in, b_in, eps0, out):
         mx_psum = ctx.enter_context(tc.psum_pool(name="mx_psum", bufs=2))
         ctx.enter_context(tc.manual_schedule())
 
-        w_raw = keep.tile([P, PACK, HID], BF16)
+        w_raw = keep.tile([P, PACK, HID], BF16, align_bytes=256)
         nc.scalar.dma_start(out=w_raw[:].rearrange("q (u e) n -> q u (e n)", u=2), in_=w_view)
         row = keep.tile([1, 2 * HID], BF16)
         nc.scalar.dma_start(out=row[:, 0:HID], in_=b_in.unsqueeze(0))
@@ -66,12 +66,12 @@ def tile_gin_pa_t_kernel(tc, X, A, W_in, b_in, eps0, out):
         nc.vector.memset(ones[:], 1.0)
 
         def load_x(x):
-            x_rows = x_pool.tile([P, SLAB_K], BF16)
+            x_rows = x_pool.tile([P, SLAB_K], BF16, align_bytes=256)
             nc.sync.dma_start(out=x_rows[:], in_=x_view[x])
             return x_rows
 
         def load_a(c):
-            a_rows = a_pool.tile([P, 2 * SLAB_K], BF16)
+            a_rows = a_pool.tile([P, 2 * SLAB_K], BF16, align_bytes=256)
             cuts = CUTS.get(c, (8,))
             first = 0
             for w in cuts:
@@ -86,12 +86,12 @@ def tile_gin_pa_t_kernel(tc, X, A, W_in, b_in, eps0, out):
         ident = keep.tile([P, P], F32)
         make_identity(nc, ident[:])
 
-        w_grouped = keep.tile([P, HID, PACK], BF16, align_bytes=64)
+        w_grouped = keep.tile([P, HID, PACK], BF16, align_bytes=256)
         nc.vector.tensor_copy(out=w_grouped[:], in_=w_raw[:].rearrange("q t n -> q n t"))
         bias = keep.tile([P, HID], F32)
         one_plus_eps = keep.tile([P, 1], F32)
-        w_codes = keep.tile([P, HID], U32, align_bytes=64)
-        w_scales = keep.tile([P, HID], U8, align_bytes=64)
+        w_codes = keep.tile([P, HID], U32, align_bytes=256)
+        w_scales = keep.tile([P, HID], U8, align_bytes=256)
         nc.vector.quantize_mx(
             out=w_codes[:].bitcast(FP8X4),
             scales=w_scales[:],
@@ -99,9 +99,9 @@ def tile_gin_pa_t_kernel(tc, X, A, W_in, b_in, eps0, out):
         )
 
         h_f32 = keep.tile([P, PASSES, PACK, HID], F32)
-        h_grouped = keep.tile([P, PASSES, HID, PACK], BF16, align_bytes=64)
-        h_codes = keep.tile([P, PASSES, HID], U32, align_bytes=64)
-        h_scales = keep.tile([P, PASSES, HID], U8, align_bytes=64)
+        h_grouped = keep.tile([P, PASSES, HID, PACK], BF16, align_bytes=256)
+        h_codes = keep.tile([P, PASSES, HID], U32, align_bytes=256)
+        h_scales = keep.tile([P, PASSES, HID], U8, align_bytes=256)
 
         def slab_words(i):
             if i < X_SLABS:
@@ -115,7 +115,7 @@ def tile_gin_pa_t_kernel(tc, X, A, W_in, b_in, eps0, out):
 
         def transpose_bank(i, j, halves=False):
             if j == 0:
-                grouped = grouped_pool.tile([P, SLAB_K], BF16, align_bytes=64)
+                grouped = grouped_pool.tile([P, SLAB_K], BF16, align_bytes=256)
                 grouped_of[i] = grouped
             words = slab_words(i)
             grouped_words = grouped_of[i][:].bitcast(F32).rearrange(
@@ -160,8 +160,8 @@ def tile_gin_pa_t_kernel(tc, X, A, W_in, b_in, eps0, out):
 
         def quantise(i, j0, j1):
             if j0 == 0:
-                codes = packed_pool.tile([P, SLAB_OPERANDS, P], U32, align_bytes=64)
-                scales = packed_pool.tile([P, SLAB_OPERANDS, P], U8, align_bytes=64)
+                codes = packed_pool.tile([P, SLAB_OPERANDS, P], U32, align_bytes=256)
+                scales = packed_pool.tile([P, SLAB_OPERANDS, P], U8, align_bytes=256)
                 packed_of[i] = (codes, scales)
             codes, scales = packed_of[i]
             ops = slice(2 * j0, 2 * j1)
@@ -251,7 +251,7 @@ def tile_gin_pa_t_kernel(tc, X, A, W_in, b_in, eps0, out):
         def finish(g, t0, t1):
             m, half = divmod(g, 2)
             if half == 0 and t0 == 0:
-                result = out_pool.tile([P, 2, PACK, HID], F32)
+                result = out_pool.tile([P, 2, PACK, HID], F32, align_bytes=256)
                 result_of[m] = result
             nc.vector.scalar_tensor_tensor(
                 out=result_of[m][:, half, t0:t1, :],

from contextlib import ExitStack

import concourse.mybir as mybir
from concourse.masks import make_identity

F32 = mybir.dt.float32
BF16 = mybir.dt.bfloat16
U32 = mybir.dt.uint32
U8 = mybir.dt.uint8
FP8X4 = mybir.dt.float8_e4m3fn_x4
ADD = mybir.AluOpType.add
MULT = mybir.AluOpType.mult

P = 128
NODES, FEATS, HID = 4096, 512, 128
PACK = 4
K_PASS = P * PACK
PASSES = NODES // K_PASS
SLAB_K = 4096
SLAB_OPERANDS = SLAB_K // K_PASS
SLAB_BANKS = 4
X_SLABS = NODES * FEATS // (P * SLAB_K)
A_SLABS = NODES // P
SLABS = X_SLABS + A_SLABS
A_LOADS = A_SLABS // 2
A_AHEAD = 4
VECTOR_BANK = 1
SLAB_QUANTISES = 2
MULTIPLY_RUN = 2
CUTS = {15: (4, 2, 2)}
FINE = 2
VSKIP = lambda i: i < 4 or i == 34
OFF = 1
CASTV = (1,)

FLOPS = 2 * NODES * FEATS * HID + 2 * NODES * NODES * HID


def tile_gin_pa_t_kernel(tc, X, A, W_in, b_in, eps0, out):
    nc = tc.nc

    x_view = X.rearrange("(x p i) k -> x p (i k)", p=P, i=8)
    a_view = A.rearrange("(c p e) k -> c p (e k)", p=P, e=2)
    w_view = W_in.rearrange("(u q e) n -> q u (e n)", u=2, q=P, e=2)
    out_view = out.rearrange("(m v p e) n -> m p v (e n)", v=4, p=P, e=2)

    with ExitStack() as ctx:
        keep = ctx.enter_context(tc.tile_pool(name="keep", bufs=1))
        x_pool = ctx.enter_context(tc.tile_pool(name="x_pool", bufs=X_SLABS))
        a_pool = ctx.enter_context(tc.tile_pool(name="a_pool", bufs=A_AHEAD + 1))
        grouped_pool = ctx.enter_context(tc.tile_pool(name="grouped_pool", bufs=3))
        packed_pool = ctx.enter_context(tc.tile_pool(name="packed_pool", bufs=4))
        out_pool = ctx.enter_context(tc.tile_pool(name="out_pool", bufs=4))
        tr_psum = ctx.enter_context(tc.psum_pool(name="tr_psum", bufs=6))
        mx_psum = ctx.enter_context(tc.psum_pool(name="mx_psum", bufs=2))
        ctx.enter_context(tc.manual_schedule())

        w_raw = keep.tile([P, PACK, HID], BF16, align_bytes=256)
        nc.scalar.dma_start(out=w_raw[:].rearrange("q (u e) n -> q u (e n)", u=2), in_=w_view)
        row = keep.tile([1, 2 * HID], BF16)
        nc.scalar.dma_start(out=row[:, 0:HID], in_=b_in.unsqueeze(0))
        nc.scalar.dma_start(out=row[:, HID : HID + 1], in_=eps0.unsqueeze(0))
        small = keep.tile([P, 2 * HID], BF16)
        nc.vector.memset(small[:], 0.0)
        ones = keep.tile([P, P], BF16)
        nc.vector.memset(ones[:], 1.0)

        def load_x(x):
            x_rows = x_pool.tile([P, SLAB_K], BF16, align_bytes=256)
            nc.sync.dma_start(out=x_rows[:], in_=x_view[x])
            return x_rows

        def load_a(c):
            a_rows = a_pool.tile([P, 2 * SLAB_K], BF16, align_bytes=256)
            cuts = CUTS.get(c, (8,))
            first = 0
            for w in cuts:
                cols = slice(first * 1024, (first + w) * 1024)
                first += w
                nc.sync.dma_start(out=a_rows[:, cols], in_=a_view[c][:, cols])
            return a_rows

        x_of = [load_x(x) for x in range(X_SLABS)]
        a_of = [load_a(c) for c in range(A_AHEAD)]

        ident = keep.tile([P, P], F32)
        make_identity(nc, ident[:])

        w_grouped = keep.tile([P, HID, PACK], BF16, align_bytes=256)
        nc.vector.tensor_copy(out=w_grouped[:], in_=w_raw[:].rearrange("q t n -> q n t"))
        bias = keep.tile([P, HID], F32)
        one_plus_eps = keep.tile([P, 1], F32)
        w_codes = keep.tile([P, HID], U32, align_bytes=256)
        w_scales = keep.tile([P, HID], U8, align_bytes=256)
        nc.vector.quantize_mx(
            out=w_codes[:].bitcast(FP8X4),
            scales=w_scales[:],
            in_=w_grouped[:].rearrange("q n t -> q (n t)"),
        )

        h_f32 = keep.tile([P, PASSES, PACK, HID], F32)
        h_grouped = keep.tile([P, PASSES, HID, PACK], BF16, align_bytes=256)
        h_codes = keep.tile([P, PASSES, HID], U32, align_bytes=256)
        h_scales = keep.tile([P, PASSES, HID], U8, align_bytes=256)

        def slab_words(i):
            if i < X_SLABS:
                return x_of[i][:].bitcast(F32)
            s = i - X_SLABS
            half = s % 2
            return a_of[s // 2][:, half * SLAB_K : (half + 1) * SLAB_K].bitcast(F32)

        grouped_of = {}
        packed_of = {}

        def transpose_bank(i, j, halves=False):
            if j == 0:
                grouped = grouped_pool.tile([P, SLAB_K], BF16, align_bytes=256)
                grouped_of[i] = grouped
            words = slab_words(i)
            grouped_words = grouped_of[i][:].bitcast(F32).rearrange(
                "q (o r u) -> q o r u", o=SLAB_OPERANDS, r=P, u=2
            )
            if halves:
                for o in range(2):
                    bank = tr_psum.tile([P, 2, 2, P], F32)
                    for u in range(2):
                        first = (4 * j + 2 * o + u) * P
                        nc.tensor.transpose(bank[:, o, u, :], words[:, first : first + P], ident[:])
                    pairs = bank[:].rearrange("q o u r -> q o r u")
                    if o == 1:
                        nc.vector.tensor_copy(out=grouped_words[:, 2 * j + o, :, :], in_=pairs[:, o, :, :])
                    else:
                        nc.scalar.copy(out=grouped_words[:, 2 * j + o, :, :], in_=pairs[:, o, :, :])
                return
            bank = tr_psum.tile([P, 2, 2, P], F32)
            if i < X_SLABS:
                e, h = divmod(j, 2)
                for s in range(2):
                    for u in range(2):
                        first = (2 * (4 * h + 2 * s + e) + u) * P
                        nc.tensor.transpose(bank[:, s, u, :], words[:, first : first + P], ident[:])
                half = grouped_of[i][:].bitcast(F32).rearrange(
                    "q (e c r h w) -> q e c r h w", e=2, c=4, r=32, h=2, w=4
                )
                nc.scalar.copy(
                    out=half[:, e, :, :, h, :],
                    in_=bank[:].rearrange("q s u (c r) -> q c r (s u)", c=4),
                )
                return
            for o in range(2):
                for u in range(2):
                    first = (4 * j + 2 * o + u) * P
                    nc.tensor.transpose(bank[:, o, u, :], words[:, first : first + P], ident[:])
            pairs = bank[:].rearrange("q o u r -> q o r u")
            if j == VECTOR_BANK and not VSKIP(i):
                nc.vector.tensor_copy(out=grouped_words[:, 2 * j : 2 * j + 2, :, :], in_=pairs)
            else:
                nc.scalar.copy(out=grouped_words[:, 2 * j : 2 * j + 2, :, :], in_=pairs)

        def quantise(i, j0, j1):
            if j0 == 0:
                codes = packed_pool.tile([P, SLAB_OPERANDS, P], U32, align_bytes=256)
                scales = packed_pool.tile([P, SLAB_OPERANDS, P], U8, align_bytes=256)
                packed_of[i] = (codes, scales)
            codes, scales = packed_of[i]
            ops = slice(2 * j0, 2 * j1)
            nc.vector.quantize_mx(
                out=codes[:, ops, :].rearrange("q o r -> q (o r)").bitcast(FP8X4),
                scales=scales[:, ops, :].rearrange("q o r -> q (o r)"),
                in_=grouped_of[i][:, 2 * j0 * K_PASS : 2 * j1 * K_PASS],
            )

        def new_sums():
            sums = mx_psum.tile([P, PACK, HID], F32)
            return sums

        def spread_constants():
            nc.vector.tensor_copy(out=small[0:1, 0 : HID + 1], in_=row[:, 0 : HID + 1])
            sums = new_sums()
            spread = sums[:].rearrange("p t n -> p (t n)")[:, 0 : 2 * HID]
            nc.tensor.matmul(spread, lhsT=ones[:], rhs=small[:], start=True, stop=True)
            nc.vector.tensor_copy(out=bias[:], in_=spread[:, 0:HID])
            nc.vector.tensor_scalar_add(
                out=one_plus_eps[:], in0=spread[:, HID : HID + 1], scalar1=1.0
            )

        def project(x, codes, scales):
            pair = []
            for g in range(2):
                sums = new_sums()
                pair.append(sums)
                for t in range(PACK):
                    u, e = divmod(t, 2)
                    o = 4 * e + 2 * g + u
                    nc.tensor.matmul_mx(
                        out=sums[:, t, :],
                        lhsT=codes[:, o, :].bitcast(FP8X4),
                        lhsT_scale=scales[:, o, :],
                        rhs=w_codes[:].bitcast(FP8X4),
                        rhs_scale=w_scales[:],
                        start=True,
                        stop=True,
                    )
            for g in range(2):
                nc.vector.tensor_tensor(
                    out=h_f32[:, 2 * x + g, :, :],
                    in0=pair[g][:],
                    in1=bias[:].unsqueeze(1).to_broadcast([P, PACK, HID]),
                    op=ADD,
                )

        def cast_h(x):
            for g in (2 * x, 2 * x + 1):
                cp = nc.vector.tensor_copy if g % 2 in CASTV else nc.scalar.copy
                cp(out=h_grouped[:, g, :, :], in_=h_f32[:, g, :, :].rearrange("p t n -> p n t"))

        def quantise_h(x):
            g_pair = slice(2 * x, 2 * x + 2)
            nc.vector.quantize_mx(
                out=h_codes[:, g_pair, :].rearrange("p g n -> p (g n)").bitcast(FP8X4),
                scales=h_scales[:, g_pair, :].rearrange("p g n -> p (g n)"),
                in_=h_grouped[:, g_pair, :, :].rearrange("p g n t -> p (g n t)"),
            )

        sums_of = {}

        def aggregate(i, g0, g1):
            if g1 <= g0:
                return
            group, t = divmod(i - X_SLABS, PACK)
            if t == 0 and g0 == 0:
                sums_of[group] = new_sums()
            if i == last and g0 == 0:
                sums_of["last"] = new_sums()
            sums = sums_of["last" if i == last else group]
            codes, scales = packed_of[i]
            for g in range(g0, g1):
                nc.tensor.matmul_mx(
                    out=sums[:, t, :],
                    lhsT=codes[:, g, :].bitcast(FP8X4),
                    lhsT_scale=scales[:, g, :],
                    rhs=h_codes[:, g, :].bitcast(FP8X4),
                    rhs_scale=h_scales[:, g, :],
                    start=(g == 0),
                    stop=(g == PASSES - 1),
                )

        result_of = {}

        def finish(g, t0, t1):
            m, half = divmod(g, 2)
            if half == 0 and t0 == 0:
                result = out_pool.tile([P, 2, PACK, HID], F32, align_bytes=256)
                result_of[m] = result
            nc.vector.scalar_tensor_tensor(
                out=result_of[m][:, half, t0:t1, :],
                in0=h_f32[:, g, t0:t1, :],
                scalar=one_plus_eps[:, 0:1],
                in1=sums_of["last" if t0 == 3 else g][:, t0:t1, :],
                op0=MULT,
                op1=ADD,
            )

        def store(m, v0, v1):
            rows = result_of[m][:].rearrange("p g (u e) n -> p (g u) (e n)", u=2)
            nc.sync.dma_start(out=out_view[m][:, v0:v1, :], in_=rows[:, v0:v1, :])

        projected = []
        queue = []
        done = 0
        last = SLABS - 1

        def multiply(hh):
            i, half = divmod(hh, 2)
            if i < X_SLABS:
                if half == 1:
                    project(i, *packed_of[i])
                return
            aggregate(i, 4 * half, 4 * half + 4)
            group, t = divmod(i - X_SLABS, PACK)
            if half == 1 and t == PACK - 1 and i < last:
                finish(group, 0, PACK)
                if group % 2 == 1:
                    waiting.append((group // 2, 0, 4))
                elif group == 6:
                    waiting.append((3, 0, 2))
                flush()

        waiting = []

        def flush():
            if len(a_of) == A_LOADS:
                for piece in waiting:
                    store(*piece)
                waiting.clear()

        def load_more(step):
            s = step - X_SLABS
            if s >= 0 and s % 2 == 0 and s // 2 + A_AHEAD < A_LOADS:
                a_of.append(load_a(s // 2 + A_AHEAD))

        X = X_SLABS
        for s in range(SLABS - 2):
            load_more(s)
            transpose_bank(s, 0)
            transpose_bank(s, 1)
            if s > 0:
                quantise(s - 1, 2, 4)
            transpose_bank(s, 2)
            if 0 <= s - 2 < X_SLABS:
                cast_h(s - 2)
            quantise(s, 0, 2)
            transpose_bank(s, 3)
            if 0 <= s - 2 < X_SLABS:
                quantise_h(s - 2)
            if s == 0:
                spread_constants()
            ready = 2 * s - OFF if s > X_SLABS else 2 * s
            run = 2 * MULTIPLY_RUN if X_SLABS + 1 < s < SLABS - FINE else 2
            if ready - done >= run:
                while done < ready:
                    multiply(done)
                    done += 1
        a, b = last - 1, last
        transpose_bank(a, 0)
        transpose_bank(a, 1)
        quantise(a - 1, 2, 4)
        transpose_bank(a, 2)
        quantise(a, 0, 2)
        transpose_bank(a, 3)
        transpose_bank(b, 0)
        transpose_bank(b, 1)
        quantise(a, 2, 4)
        transpose_bank(b, 2)
        quantise(b, 0, 2)
        while done < 2 * a + 1:
            multiply(done)
            done += 1
        transpose_bank(b, 3, True)
        quantise(b, 2, 3)
        multiply(done)
        done += 1
        quantise(b, 3, 4)
        aggregate(b, 0, 6)
        finish(7, 0, 3)
        store(3, 2, 3)
        aggregate(b, 6, 8)
        finish(7, 3, 4)
        store(3, 3, 4)
